import numpy as np
import ml_dtypes


def mxq(x, axis, fmt="e4m3"):
    dtype, down = {"e4m3": (ml_dtypes.float8_e4m3fn, 7), "e5m2": (ml_dtypes.float8_e5m2, 14)}[fmt]
    v = np.moveaxis(np.asarray(x, np.float32).astype(ml_dtypes.bfloat16).astype(np.float64), axis, -1)
    blocks = v.reshape(v.shape[:-1] + (-1, 32))
    amax = np.abs(blocks).max(-1, keepdims=True)
    byte = np.maximum(np.where(amax > 0, np.frexp(amax)[1] - 1 + 127, 0) - down, 1)
    scale = np.exp2(byte - 127.0)
    codes = (blocks / scale).astype(np.float32).astype(dtype).astype(np.float64)
    return np.moveaxis((codes * scale).reshape(v.shape), -1, axis)


WIDE = False


def mx_kscale(k):
    if not WIDE:
        return np.ones(k)
    levels = np.array([10, -10, 5, -5, 0])
    a = np.random.permutation(np.resize(levels, k // 512 * 4)).reshape(k // 512, 4)
    idx = np.arange(k)
    return np.exp2(a[idx // 512, idx % 128 // 32])


BF16 = ml_dtypes.bfloat16


def bf(x):
    return np.asarray(x, np.float32).astype(BF16)


def f64(x):
    return np.asarray(x).astype(np.float64)


N_V, N_E, N_F, D_IN, D_OUT = 1536, 3072, 2048, 128, 128
LIM = np.sqrt(6.0 / (D_IN + D_OUT))


def glorot():
    return np.random.uniform(-LIM, LIM, (D_IN, D_OUT))


def setup_inputs():
    se, sf = mx_kscale(N_E), mx_kscale(N_F)
    return {"xe": bf(np.random.standard_normal((N_E, D_IN)) / se[:, None]),
            "xf": bf(np.random.standard_normal((N_F, D_IN)) / sf[:, None]),
            "Ge2f": bf(np.random.standard_normal((N_F, N_E)) / np.sqrt(N_E) * se),
            "Gf2f": bf(np.random.standard_normal((N_F, N_F)) / np.sqrt(N_F) * sf),
            "We2f": bf(glorot()), "Wf2f": bf(glorot())}


def reference(xe, xf, Ge2f, Gf2f, We2f, Wf2f):
    he2f = f64(xe) @ f64(We2f)
    hf2f = f64(xf) @ f64(Wf2f)
    return (mxq(f64(Ge2f), 1, "e4m3") @ mxq(he2f, 0, "e4m3")) + (mxq(f64(Gf2f), 1, "e4m3") @ mxq(hf2f, 0, "e4m3"))

@@ -1,0 +1,190 @@
+from contextlib import ExitStack
+
+import concourse.mybir as mybir
+from concourse.masks import make_identity
+
+BF16 = mybir.dt.bfloat16
+F32 = mybir.dt.float32
+U32 = mybir.dt.uint32
+U8 = mybir.dt.uint8
+FP8X4 = mybir.dt.float8_e4m3fn_x4
+
+P = 128
+PACK = 4
+K_PASS = P * PACK
+N_E, N_F, D = 3072, 2048, 128
+E_PASSES = N_E // K_PASS
+F_PASSES = N_F // K_PASS
+PASSES = E_PASSES + F_PASSES
+WORDS_PASS = K_PASS // 2
+
+ROW_TILES = 2
+ROUND_ROWS = ROW_TILES * P
+ROUNDS = N_F // ROUND_ROWS
+CHUNK_PASSES = 2
+CHUNKS = PASSES // CHUNK_PASSES
+G_CHUNK = CHUNK_PASSES * ROW_TILES * K_PASS
+H_CHUNK = CHUNK_PASSES * K_PASS
+
+G_BUFS = 6
+WORK_BANKS = 6
+VECTOR_BANK_EVERY = 5
+
+FLOPS = 2 * N_F * (N_E + N_F) * D + 2 * (N_E + N_F) * D * D
+
+
+def tile_two_d_cxn_cmps_pb_kernel(tc, xe, xf, Ge2f, Gf2f, We2f, Wf2f, out):
+    nc = tc.nc
+    with ExitStack() as stack:
+        keep = stack.enter_context(tc.tile_pool(name="keep", bufs=1))
+        g_pool = stack.enter_context(tc.tile_pool(name="g", bufs=G_BUFS))
+        grouped_pool = stack.enter_context(tc.tile_pool(name="grouped", bufs=4))
+        quantised_pool = stack.enter_context(tc.tile_pool(name="quantised", bufs=3))
+        z_pool = stack.enter_context(tc.tile_pool(name="z", bufs=3))
+        work = stack.enter_context(tc.psum_pool(name="work", bufs=WORK_BANKS))
+        sums = stack.enter_context(tc.psum_pool(name="sums", bufs=1))
+        stack.enter_context(tc.manual_schedule())
+
+        x_sb = keep.tile([P, PASSES * PACK, D], BF16)
+        x_pairs = x_sb[:].rearrange("p (a e) d -> p a e d", e=2)
+        for x_dram, first_pass, passes in ((xe, 0, E_PASSES), (xf, E_PASSES, F_PASSES)):
+            pairs_dram = x_dram.rearrange("(a p e) d -> p a e d", p=P, e=2)
+            for g in range(0, passes, CHUNK_PASSES):
+                nc.sync.dma_start(
+                    out=x_pairs[:, 2 * (first_pass + g) : 2 * (first_pass + g + CHUNK_PASSES)],
+                    in_=pairs_dram[:, 2 * g : 2 * (g + CHUNK_PASSES)],
+                )
+        we_sb = keep.tile([P, D], BF16)
+        nc.sync.dma_start(out=we_sb[:], in_=We2f)
+        wf_sb = keep.tile([P, D], BF16)
+        nc.sync.dma_start(out=wf_sb[:], in_=Wf2f)
+
+        def load_round(r):
+            rows = slice(r * ROUND_ROWS, (r + 1) * ROUND_ROWS)
+            ge = g_pool.tile([P, ROW_TILES, N_E], BF16)
+            nc.sync.dma_start(out=ge[:], in_=Ge2f[rows, :].rearrange("(p j) k -> p j k", j=ROW_TILES))
+            gf = g_pool.tile([P, ROW_TILES, N_F], BF16)
+            nc.sync.dma_start(out=gf[:], in_=Gf2f[rows, :].rearrange("(p j) k -> p j k", j=ROW_TILES))
+            return ge[:].bitcast(F32), gf[:].bitcast(F32)
+
+        g_words = {}
+        for r in range(G_BUFS):
+            g_words[r] = load_round(r)
+
+        ident_bf16 = keep.tile([P, P], BF16)
+        make_identity(nc, ident_bf16[:])
+        ident_f32 = keep.tile([P, P], F32)
+        make_identity(nc, ident_f32[:])
+
+        def copy_out(g, dst, src):
+            if g % 2 == 0:
+                nc.scalar.copy(out=dst, in_=src)
+            else:
+                nc.vector.tensor_copy(out=dst, in_=src)
+
+        xT_sb = keep.tile([P, PASSES, PACK, P], BF16)
+        for g in range(PASSES):
+            xT_bank = work.tile([P, PACK, P], BF16, tag="bank")
+            for t in range(PACK):
+                nc.tensor.transpose(xT_bank[:, t, :], x_sb[:, PACK * g + t, :], ident_bf16[:])
+            copy_out(g, xT_sb[:, g], xT_bank[:])
+
+        h_grouped = keep.tile([P, PASSES, D, PACK], BF16, align_bytes=64)
+        h_codes = keep.tile([P, PASSES * D], U32, align_bytes=64)
+        h_scales = keep.tile([P, PASSES * D], U8, align_bytes=64)
+
+        def quantise_h(c):
+            cols = slice(c * CHUNK_PASSES * D, (c + 1) * CHUNK_PASSES * D)
+            nc.vector.quantize_mx(
+                out=h_codes[:, cols].bitcast(FP8X4),
+                scales=h_scales[:, cols],
+                in_=h_grouped[:, c * CHUNK_PASSES : (c + 1) * CHUNK_PASSES].rearrange(
+                    "p g d t -> p (g d t)"
+                ),
+            )
+
+        for g in range(PASSES):
+            w_sb = we_sb if g < E_PASSES else wf_sb
+            h_bank = work.tile([P, PACK, D], F32, tag="bank")
+            for t in range(PACK):
+                nc.tensor.matmul(
+                    h_bank[:, t, :], lhsT=xT_sb[:, g, t, :], rhs=w_sb[:], start=True, stop=True
+                )
+            copy_out(g, h_grouped[:, g], h_bank[:].rearrange("p t d -> p d t"))
+            if g % CHUNK_PASSES == CHUNK_PASSES - 1 and g // CHUNK_PASSES >= 1:
+                quantise_h(g // CHUNK_PASSES - 1)
+        quantise_h(CHUNKS - 1)
+
+        def operand_cols(g, j):
+            first = (g * ROW_TILES + j) * P
+            return slice(first, first + P)
+
+        def transpose_and_quantise(r):
+            ge_words, gf_words = g_words[r]
+            codes = quantised_pool.tile([P, PASSES * ROW_TILES * P], U32, align_bytes=64)
+            scales = quantised_pool.tile([P, PASSES * ROW_TILES * P], U8, align_bytes=64)
+            grouped_of = {}
+
+            def quantise(c):
+                cols = slice(c * G_CHUNK // PACK, (c + 1) * G_CHUNK // PACK)
+                nc.vector.quantize_mx(
+                    out=codes[:, cols].bitcast(FP8X4),
+                    scales=scales[:, cols],
+                    in_=grouped_of[c][:],
+                )
+
+            for c in range(CHUNKS):
+                grouped = grouped_pool.tile([P, G_CHUNK], BF16, align_bytes=64)
+                grouped_of[c] = grouped
+                grouped_words = grouped[:].bitcast(F32).rearrange(
+                    "p (g j r u) -> p g j r u", g=CHUNK_PASSES, j=ROW_TILES, u=2
+                )
+                for g in range(c * CHUNK_PASSES, (c + 1) * CHUNK_PASSES):
+                    words, g_local = (ge_words, g) if g < E_PASSES else (gf_words, g - E_PASSES)
+                    bank = work.tile([P, ROW_TILES, 2, P], F32, tag="bank")
+                    for j in range(ROW_TILES):
+                        for u in range(2):
+                            first = g_local * WORDS_PASS + u * P
+                            nc.tensor.transpose(
+                                bank[:, j, u, :], words[:, j, first : first + P], ident_f32[:]
+                            )
+                    dst = grouped_words[:, g - c * CHUNK_PASSES]
+                    src = bank[:].rearrange("p j u r -> p j r u")
+                    if g % VECTOR_BANK_EVERY == 0:
+                        nc.vector.tensor_copy(out=dst, in_=src)
+                    else:
+                        nc.scalar.copy(out=dst, in_=src)
+                if c >= 1:
+                    quantise(c - 1)
+            quantise(CHUNKS - 1)
+            return codes, scales
+
+        def multiply_and_store(r, codes, scales):
+            acc = [sums.tile([P, D], F32, name="acc%d" % j) for j in range(ROW_TILES)]
+            for g in range(PASSES):
+                h_cols = slice(g * D, (g + 1) * D)
+                for j in range(ROW_TILES):
+                    nc.tensor.matmul_mx(
+                        out=acc[j][:],
+                        lhsT=codes[:, operand_cols(g, j)].bitcast(FP8X4),
+                        lhsT_scale=scales[:, operand_cols(g, j)],
+                        rhs=h_codes[:, h_cols].bitcast(FP8X4),
+                        rhs_scale=h_scales[:, h_cols],
+                        start=(g == 0),
+                        stop=(g == PASSES - 1),
+                    )
+            z = z_pool.tile([P, ROW_TILES, D], F32)
+            nc.vector.tensor_copy(out=z[:, 0, :], in_=acc[0][:])
+            nc.scalar.copy(out=z[:, 1, :], in_=acc[1][:])
+            rows = slice(r * ROUND_ROWS, (r + 1) * ROUND_ROWS)
+            nc.sync.dma_start(out=out[rows, :].rearrange("(p j) d -> p j d", j=ROW_TILES), in_=z[:])
+
+        quantised = {}
+        for r in range(ROUNDS + 1):
+            if r < ROUNDS:
+                quantised[r] = transpose_and_quantise(r)
+                if r + G_BUFS < ROUNDS:
+                    g_words[r + G_BUFS] = load_round(r + G_BUFS)
+            if r >= 1:
+                codes, scales = quantised[r - 1]
+                multiply_and_store(r - 1, codes, scales)

@@ -23,8 +23,11 @@ ROUND_ROWS = ROW_TILES * P
 ROUNDS = N_F // ROUND_ROWS
 CHUNK_PASSES = 2
 CHUNKS = PASSES // CHUNK_PASSES
-G_CHUNK = CHUNK_PASSES * ROW_TILES * K_PASS
-H_CHUNK = CHUNK_PASSES * K_PASS
+
+STEPS = ROUNDS * PASSES
+STEP_COLS = ROW_TILES * K_PASS
+RUN_STEPS = 5
+RUNS = STEPS // RUN_STEPS
 
 G_BUFS = 6
 WORK_BANKS = 6
@@ -38,7 +41,7 @@ def tile_two_d_cxn_cmps_pb_kernel(tc, xe, xf, Ge2f, Gf2f, We2f, Wf2f, out):
     with ExitStack() as stack:
         keep = stack.enter_context(tc.tile_pool(name="keep", bufs=1))
         g_pool = stack.enter_context(tc.tile_pool(name="g", bufs=G_BUFS))
-        grouped_pool = stack.enter_context(tc.tile_pool(name="grouped", bufs=4))
+        grouped_pool = stack.enter_context(tc.tile_pool(name="grouped", bufs=6))
         quantised_pool = stack.enter_context(tc.tile_pool(name="quantised", bufs=3))
         z_pool = stack.enter_context(tc.tile_pool(name="z", bufs=3))
         work = stack.enter_context(tc.psum_pool(name="work", bufs=WORK_BANKS))
@@ -119,72 +122,78 @@ def tile_two_d_cxn_cmps_pb_kernel(tc, xe, xf, Ge2f, Gf2f, We2f, Wf2f, out):
             first = (g * ROW_TILES + j) * P
             return slice(first, first + P)
 
-        def transpose_and_quantise(r):
-            ge_words, gf_words = g_words[r]
-            codes = quantised_pool.tile([P, PASSES * ROW_TILES * P], U32, align_bytes=64)
-            scales = quantised_pool.tile([P, PASSES * ROW_TILES * P], U8, align_bytes=64)
-            grouped_of = {}
-
-            def quantise(c):
-                cols = slice(c * G_CHUNK // PACK, (c + 1) * G_CHUNK // PACK)
-                nc.vector.quantize_mx(
-                    out=codes[:, cols].bitcast(FP8X4),
-                    scales=scales[:, cols],
-                    in_=grouped_of[c][:],
-                )
-
-            for c in range(CHUNKS):
-                grouped = grouped_pool.tile([P, G_CHUNK], BF16, align_bytes=64)
-                grouped_of[c] = grouped
-                grouped_words = grouped[:].bitcast(F32).rearrange(
-                    "p (g j r u) -> p g j r u", g=CHUNK_PASSES, j=ROW_TILES, u=2
-                )
-                for g in range(c * CHUNK_PASSES, (c + 1) * CHUNK_PASSES):
-                    words, g_local = (ge_words, g) if g < E_PASSES else (gf_words, g - E_PASSES)
-                    bank = work.tile([P, ROW_TILES, 2, P], F32, tag="bank")
-                    for j in range(ROW_TILES):
-                        for u in range(2):
-                            first = g_local * WORDS_PASS + u * P
-                            nc.tensor.transpose(
-                                bank[:, j, u, :], words[:, j, first : first + P], ident_f32[:]
-                            )
-                    dst = grouped_words[:, g - c * CHUNK_PASSES]
-                    src = bank[:].rearrange("p j u r -> p j r u")
-                    if g % VECTOR_BANK_EVERY == 0:
-                        nc.vector.tensor_copy(out=dst, in_=src)
-                    else:
-                        nc.scalar.copy(out=dst, in_=src)
-                if c >= 1:
-                    quantise(c - 1)
-            quantise(CHUNKS - 1)
-            return codes, scales
-
-        def multiply_and_store(r, codes, scales):
-            acc = [sums.tile([P, D], F32, name="acc%d" % j) for j in range(ROW_TILES)]
-            for g in range(PASSES):
-                h_cols = slice(g * D, (g + 1) * D)
-                for j in range(ROW_TILES):
-                    nc.tensor.matmul_mx(
-                        out=acc[j][:],
-                        lhsT=codes[:, operand_cols(g, j)].bitcast(FP8X4),
-                        lhsT_scale=scales[:, operand_cols(g, j)],
-                        rhs=h_codes[:, h_cols].bitcast(FP8X4),
-                        rhs_scale=h_scales[:, h_cols],
-                        start=(g == 0),
-                        stop=(g == PASSES - 1),
-                    )
-            z = z_pool.tile([P, ROW_TILES, D], F32)
-            nc.vector.tensor_copy(out=z[:, 0, :], in_=acc[0][:])
-            nc.scalar.copy(out=z[:, 1, :], in_=acc[1][:])
-            rows = slice(r * ROUND_ROWS, (r + 1) * ROUND_ROWS)
-            nc.sync.dma_start(out=out[rows, :].rearrange("(p j) d -> p j d", j=ROW_TILES), in_=z[:])
-
         quantised = {}
-        for r in range(ROUNDS + 1):
-            if r < ROUNDS:
-                quantised[r] = transpose_and_quantise(r)
-                if r + G_BUFS < ROUNDS:
-                    g_words[r + G_BUFS] = load_round(r + G_BUFS)
-            if r >= 1:
-                codes, scales = quantised[r - 1]
-                multiply_and_store(r - 1, codes, scales)
+        grouped_of = {}
+        acc_of = {}
+
+        def transpose_step(s):
+            r, g = divmod(s, PASSES)
+            if g == 0:
+                codes = quantised_pool.tile([P, PASSES * ROW_TILES * P], U32, align_bytes=64)
+                scales = quantised_pool.tile([P, PASSES * ROW_TILES * P], U8, align_bytes=64)
+                quantised[r] = (codes, scales)
+            ge_words, gf_words = g_words[r]
+            words, g_local = (ge_words, g) if g < E_PASSES else (gf_words, g - E_PASSES)
+            bank = work.tile([P, ROW_TILES, 2, P], F32, tag="bank")
+            for j in range(ROW_TILES):
+                for u in range(2):
+                    first = g_local * WORDS_PASS + u * P
+                    nc.tensor.transpose(
+                        bank[:, j, u, :], words[:, j, first : first + P], ident_f32[:]
+                    )
+            grouped = grouped_pool.tile([P, STEP_COLS], BF16, align_bytes=64)
+            grouped_of[s] = grouped
+            dst = grouped[:].bitcast(F32).rearrange("p (j r u) -> p j r u", j=ROW_TILES, u=2)
+            src = bank[:].rearrange("p j u r -> p j r u")
+            if s % VECTOR_BANK_EVERY == 0:
+                nc.vector.tensor_copy(out=dst, in_=src)
+            else:
+                nc.scalar.copy(out=dst, in_=src)
+            if g == PASSES - 1 and r + G_BUFS < ROUNDS:
+                g_words[r + G_BUFS] = load_round(r + G_BUFS)
+
+        def quantise_step(s):
+            r, g = divmod(s, PASSES)
+            codes, scales = quantised[r]
+            cols = slice(g * ROW_TILES * P, (g + 1) * ROW_TILES * P)
+            nc.vector.quantize_mx(
+                out=codes[:, cols].bitcast(FP8X4), scales=scales[:, cols], in_=grouped_of[s][:]
+            )
+
+        def multiply_step(s):
+            r, g = divmod(s, PASSES)
+            codes, scales = quantised[r]
+            if g == 0:
+                acc_of[r] = [sums.tile([P, D], F32, name="acc%d" % j) for j in range(ROW_TILES)]
+            acc = acc_of[r]
+            h_cols = slice(g * D, (g + 1) * D)
+            for j in range(ROW_TILES):
+                nc.tensor.matmul_mx(
+                    out=acc[j][:],
+                    lhsT=codes[:, operand_cols(g, j)].bitcast(FP8X4),
+                    lhsT_scale=scales[:, operand_cols(g, j)],
+                    rhs=h_codes[:, h_cols].bitcast(FP8X4),
+                    rhs_scale=h_scales[:, h_cols],
+                    start=(g == 0),
+                    stop=(g == PASSES - 1),
+                )
+            if g == PASSES - 1:
+                z = z_pool.tile([P, ROW_TILES, D], F32)
+                nc.vector.tensor_copy(out=z[:, 0, :], in_=acc[0][:])
+                nc.scalar.copy(out=z[:, 1, :], in_=acc[1][:])
+                rows = slice(r * ROUND_ROWS, (r + 1) * ROUND_ROWS)
+                nc.sync.dma_start(
+                    out=out[rows, :].rearrange("(p j) d -> p j d", j=ROW_TILES), in_=z[:]
+                )
+
+        for run in range(RUNS + 1):
+            if run < RUNS:
+                for s in range(run * RUN_STEPS, (run + 1) * RUN_STEPS):
+                    transpose_step(s)
+                    if s >= 1:
+                        quantise_step(s - 1)
+            else:
+                quantise_step(STEPS - 1)
+            if run >= 1:
+                for s in range((run - 1) * RUN_STEPS, run * RUN_STEPS):
+                    multiply_step(s)

@@ -43,7 +43,7 @@ def tile_two_d_cxn_cmps_pb_kernel(tc, xe, xf, Ge2f, Gf2f, We2f, Wf2f, out):
         g_pool = stack.enter_context(tc.tile_pool(name="g", bufs=G_BUFS))
         grouped_pool = stack.enter_context(tc.tile_pool(name="grouped", bufs=6))
         quantised_pool = stack.enter_context(tc.tile_pool(name="quantised", bufs=3))
-        z_pool = stack.enter_context(tc.tile_pool(name="z", bufs=3))
+        z_pool = stack.enter_context(tc.tile_pool(name="z", bufs=ROUNDS))
         work = stack.enter_context(tc.psum_pool(name="work", bufs=WORK_BANKS))
         sums = stack.enter_context(tc.psum_pool(name="sums", bufs=1))
         stack.enter_context(tc.manual_schedule())

@@ -23,6 +23,7 @@ ROUND_ROWS = ROW_TILES * P
 ROUNDS = N_F // ROUND_ROWS
 CHUNK_PASSES = 2
 CHUNKS = PASSES // CHUNK_PASSES
+X_AHEAD = 2
 
 STEPS = ROUNDS * PASSES
 STEP_COLS = ROW_TILES * K_PASS
@@ -48,6 +49,10 @@ def tile_two_d_cxn_cmps_pb_kernel(tc, xe, xf, Ge2f, Gf2f, We2f, Wf2f, out):
         sums = stack.enter_context(tc.psum_pool(name="sums", bufs=1))
         stack.enter_context(tc.manual_schedule())
 
+        we_sb = keep.tile([P, D], BF16)
+        nc.sync.dma_start(out=we_sb[:], in_=We2f)
+        wf_sb = keep.tile([P, D], BF16)
+        nc.sync.dma_start(out=wf_sb[:], in_=Wf2f)
         x_sb = keep.tile([P, PASSES * PACK, D], BF16)
         x_pairs = x_sb[:].rearrange("p (a e) d -> p a e d", e=2)
         for x_dram, first_pass, passes in ((xe, 0, E_PASSES), (xf, E_PASSES, F_PASSES)):
@@ -57,11 +62,6 @@ def tile_two_d_cxn_cmps_pb_kernel(tc, xe, xf, Ge2f, Gf2f, We2f, Wf2f, out):
                     out=x_pairs[:, 2 * (first_pass + g) : 2 * (first_pass + g + CHUNK_PASSES)],
                     in_=pairs_dram[:, 2 * g : 2 * (g + CHUNK_PASSES)],
                 )
-        we_sb = keep.tile([P, D], BF16)
-        nc.sync.dma_start(out=we_sb[:], in_=We2f)
-        wf_sb = keep.tile([P, D], BF16)
-        nc.sync.dma_start(out=wf_sb[:], in_=Wf2f)
-
         def load_round(r):
             rows = slice(r * ROUND_ROWS, (r + 1) * ROUND_ROWS)
             ge = g_pool.tile([P, ROW_TILES, N_E], BF16)
@@ -79,22 +79,31 @@ def tile_two_d_cxn_cmps_pb_kernel(tc, xe, xf, Ge2f, Gf2f, We2f, Wf2f, out):
         ident_f32 = keep.tile([P, P], F32)
         make_identity(nc, ident_f32[:])
 
-        def copy_out(g, dst, src):
-            if g % 2 == 0:
+        xT_sb = keep.tile([P, PASSES, PACK, P], BF16)
+        h_grouped = keep.tile([P, PASSES, D, PACK], BF16, align_bytes=64)
+        h_codes = keep.tile([P, PASSES * D], U32, align_bytes=64)
+        h_scales = keep.tile([P, PASSES * D], U8, align_bytes=64)
+
+        def copy_out(on_scalar, dst, src):
+            if on_scalar:
                 nc.scalar.copy(out=dst, in_=src)
             else:
                 nc.vector.tensor_copy(out=dst, in_=src)
 
-        xT_sb = keep.tile([P, PASSES, PACK, P], BF16)
-        for g in range(PASSES):
+        def transpose_x(g):
             xT_bank = work.tile([P, PACK, P], BF16, tag="bank")
             for t in range(PACK):
                 nc.tensor.transpose(xT_bank[:, t, :], x_sb[:, PACK * g + t, :], ident_bf16[:])
-            copy_out(g, xT_sb[:, g], xT_bank[:])
+            copy_out(g % 2 == 0, xT_sb[:, g], xT_bank[:])
 
-        h_grouped = keep.tile([P, PASSES, D, PACK], BF16, align_bytes=64)
-        h_codes = keep.tile([P, PASSES * D], U32, align_bytes=64)
-        h_scales = keep.tile([P, PASSES * D], U8, align_bytes=64)
+        def multiply_x(g):
+            w_sb = we_sb if g < E_PASSES else wf_sb
+            h_bank = work.tile([P, PACK, D], F32, tag="bank")
+            for t in range(PACK):
+                nc.tensor.matmul(
+                    h_bank[:, t, :], lhsT=xT_sb[:, g, t, :], rhs=w_sb[:], start=True, stop=True
+                )
+            copy_out(g % 2 == 1, h_grouped[:, g], h_bank[:].rearrange("p t d -> p d t"))
 
         def quantise_h(c):
             cols = slice(c * CHUNK_PASSES * D, (c + 1) * CHUNK_PASSES * D)
@@ -106,14 +115,12 @@ def tile_two_d_cxn_cmps_pb_kernel(tc, xe, xf, Ge2f, Gf2f, We2f, Wf2f, out):
                 ),
             )
 
+        for g in range(X_AHEAD):
+            transpose_x(g)
         for g in range(PASSES):
-            w_sb = we_sb if g < E_PASSES else wf_sb
-            h_bank = work.tile([P, PACK, D], F32, tag="bank")
-            for t in range(PACK):
-                nc.tensor.matmul(
-                    h_bank[:, t, :], lhsT=xT_sb[:, g, t, :], rhs=w_sb[:], start=True, stop=True
-                )
-            copy_out(g, h_grouped[:, g], h_bank[:].rearrange("p t d -> p d t"))
+            if g + X_AHEAD < PASSES:
+                transpose_x(g + X_AHEAD)
+            multiply_x(g)
             if g % CHUNK_PASSES == CHUNK_PASSES - 1 and g // CHUNK_PASSES >= 1:
                 quantise_h(g // CHUNK_PASSES - 1)
         quantise_h(CHUNKS - 1)

@@ -17,22 +17,16 @@ E_PASSES = N_E // K_PASS
 F_PASSES = N_F // K_PASS
 PASSES = E_PASSES + F_PASSES
 WORDS_PASS = K_PASS // 2
+ROUNDS = N_F // P
 
-ROW_TILES = 2
-ROUND_ROWS = ROW_TILES * P
-ROUNDS = N_F // ROUND_ROWS
-CHUNK_PASSES = 2
-CHUNKS = PASSES // CHUNK_PASSES
+STEP_PASSES = 2
+STEPS = PASSES // STEP_PASSES
+STEP_COLS = STEP_PASSES * K_PASS
+STEP_WORDS = STEP_COLS // PACK
+
 X_AHEAD = 2
-
-STEPS = ROUNDS * PASSES
-STEP_COLS = ROW_TILES * K_PASS
-RUN_STEPS = 5
-RUNS = STEPS // RUN_STEPS
-
-G_BUFS = 6
+G_BUFS = 14
 WORK_BANKS = 6
-VECTOR_BANK_EVERY = 5
 
 FLOPS = 2 * N_F * (N_E + N_F) * D + 2 * (N_E + N_F) * D * D
 
@@ -43,10 +37,10 @@ def tile_two_d_cxn_cmps_pb_kernel(tc, xe, xf, Ge2f, Gf2f, We2f, Wf2f, out):
         keep = stack.enter_context(tc.tile_pool(name="keep", bufs=1))
         g_pool = stack.enter_context(tc.tile_pool(name="g", bufs=G_BUFS))
         grouped_pool = stack.enter_context(tc.tile_pool(name="grouped", bufs=6))
-        quantised_pool = stack.enter_context(tc.tile_pool(name="quantised", bufs=3))
+        quantised_pool = stack.enter_context(tc.tile_pool(name="quantised", bufs=4))
         z_pool = stack.enter_context(tc.tile_pool(name="z", bufs=ROUNDS))
         work = stack.enter_context(tc.psum_pool(name="work", bufs=WORK_BANKS))
-        sums = stack.enter_context(tc.psum_pool(name="sums", bufs=1))
+        sums = stack.enter_context(tc.psum_pool(name="sums", bufs=2))
         stack.enter_context(tc.manual_schedule())
 
         we_sb = keep.tile([P, D], BF16)
@@ -57,17 +51,18 @@ def tile_two_d_cxn_cmps_pb_kernel(tc, xe, xf, Ge2f, Gf2f, We2f, Wf2f, out):
         x_pairs = x_sb[:].rearrange("p (a e) d -> p a e d", e=2)
         for x_dram, first_pass, passes in ((xe, 0, E_PASSES), (xf, E_PASSES, F_PASSES)):
             pairs_dram = x_dram.rearrange("(a p e) d -> p a e d", p=P, e=2)
-            for g in range(0, passes, CHUNK_PASSES):
+            for g in range(0, passes, STEP_PASSES):
                 nc.sync.dma_start(
-                    out=x_pairs[:, 2 * (first_pass + g) : 2 * (first_pass + g + CHUNK_PASSES)],
-                    in_=pairs_dram[:, 2 * g : 2 * (g + CHUNK_PASSES)],
+                    out=x_pairs[:, 2 * (first_pass + g) : 2 * (first_pass + g + STEP_PASSES)],
+                    in_=pairs_dram[:, 2 * g : 2 * (g + STEP_PASSES)],
                 )
+
         def load_round(r):
-            rows = slice(r * ROUND_ROWS, (r + 1) * ROUND_ROWS)
-            ge = g_pool.tile([P, ROW_TILES, N_E], BF16)
-            nc.sync.dma_start(out=ge[:], in_=Ge2f[rows, :].rearrange("(p j) k -> p j k", j=ROW_TILES))
-            gf = g_pool.tile([P, ROW_TILES, N_F], BF16)
-            nc.sync.dma_start(out=gf[:], in_=Gf2f[rows, :].rearrange("(p j) k -> p j k", j=ROW_TILES))
+            rows = slice(r * P, (r + 1) * P)
+            ge = g_pool.tile([P, N_E], BF16)
+            nc.sync.dma_start(out=ge[:], in_=Ge2f[rows, :])
+            gf = g_pool.tile([P, N_F], BF16)
+            nc.sync.dma_start(out=gf[:], in_=Gf2f[rows, :])
             return ge[:].bitcast(F32), gf[:].bitcast(F32)
 
         g_words = {}
@@ -106,11 +101,11 @@ def tile_two_d_cxn_cmps_pb_kernel(tc, xe, xf, Ge2f, Gf2f, We2f, Wf2f, out):
             copy_out(g % 2 == 1, h_grouped[:, g], h_bank[:].rearrange("p t d -> p d t"))
 
         def quantise_h(c):
-            cols = slice(c * CHUNK_PASSES * D, (c + 1) * CHUNK_PASSES * D)
+            cols = slice(c * STEP_WORDS, (c + 1) * STEP_WORDS)
             nc.vector.quantize_mx(
                 out=h_codes[:, cols].bitcast(FP8X4),
                 scales=h_scales[:, cols],
-                in_=h_grouped[:, c * CHUNK_PASSES : (c + 1) * CHUNK_PASSES].rearrange(
+                in_=h_grouped[:, c * STEP_PASSES : (c + 1) * STEP_PASSES].rearrange(
                     "p g d t -> p (g d t)"
                 ),
             )
@@ -121,86 +116,68 @@ def tile_two_d_cxn_cmps_pb_kernel(tc, xe, xf, Ge2f, Gf2f, We2f, Wf2f, out):
             if g + X_AHEAD < PASSES:
                 transpose_x(g + X_AHEAD)
             multiply_x(g)
-            if g % CHUNK_PASSES == CHUNK_PASSES - 1 and g // CHUNK_PASSES >= 1:
-                quantise_h(g // CHUNK_PASSES - 1)
-        quantise_h(CHUNKS - 1)
-
-        def operand_cols(g, j):
-            first = (g * ROW_TILES + j) * P
-            return slice(first, first + P)
+            if g % STEP_PASSES == STEP_PASSES - 1 and g // STEP_PASSES >= 1:
+                quantise_h(g // STEP_PASSES - 1)
+        quantise_h(STEPS - 1)
 
         quantised = {}
         grouped_of = {}
-        acc_of = {}
 
-        def transpose_step(s):
-            r, g = divmod(s, PASSES)
-            if g == 0:
-                codes = quantised_pool.tile([P, PASSES * ROW_TILES * P], U32, align_bytes=64)
-                scales = quantised_pool.tile([P, PASSES * ROW_TILES * P], U8, align_bytes=64)
-                quantised[r] = (codes, scales)
+        def transpose_step(r, c):
             ge_words, gf_words = g_words[r]
-            words, g_local = (ge_words, g) if g < E_PASSES else (gf_words, g - E_PASSES)
-            bank = work.tile([P, ROW_TILES, 2, P], F32, tag="bank")
-            for j in range(ROW_TILES):
+            bank = work.tile([P, STEP_PASSES, 2, P], F32, tag="bank")
+            for i in range(STEP_PASSES):
+                g = c * STEP_PASSES + i
+                words, g_local = (ge_words, g) if g < E_PASSES else (gf_words, g - E_PASSES)
                 for u in range(2):
                     first = g_local * WORDS_PASS + u * P
-                    nc.tensor.transpose(
-                        bank[:, j, u, :], words[:, j, first : first + P], ident_f32[:]
-                    )
+                    nc.tensor.transpose(bank[:, i, u, :], words[:, first : first + P], ident_f32[:])
             grouped = grouped_pool.tile([P, STEP_COLS], BF16, align_bytes=64)
-            grouped_of[s] = grouped
-            dst = grouped[:].bitcast(F32).rearrange("p (j r u) -> p j r u", j=ROW_TILES, u=2)
-            src = bank[:].rearrange("p j u r -> p j r u")
-            if s % VECTOR_BANK_EVERY == 0:
-                nc.vector.tensor_copy(out=dst, in_=src)
-            else:
-                nc.scalar.copy(out=dst, in_=src)
-            if g == PASSES - 1 and r + G_BUFS < ROUNDS:
-                g_words[r + G_BUFS] = load_round(r + G_BUFS)
+            grouped_of[(r, c)] = grouped
+            dst = grouped[:].bitcast(F32).rearrange("p (i r u) -> p i r u", i=STEP_PASSES, u=2)
+            copy_out(c != 0, dst, bank[:].rearrange("p i u r -> p i r u"))
 
-        def quantise_step(s):
-            r, g = divmod(s, PASSES)
+        def quantise_step(r, c):
             codes, scales = quantised[r]
-            cols = slice(g * ROW_TILES * P, (g + 1) * ROW_TILES * P)
+            cols = slice(c * STEP_WORDS, (c + 1) * STEP_WORDS)
             nc.vector.quantize_mx(
-                out=codes[:, cols].bitcast(FP8X4), scales=scales[:, cols], in_=grouped_of[s][:]
+                out=codes[:, cols].bitcast(FP8X4), scales=scales[:, cols], in_=grouped_of[(r, c)][:]
             )
 
-        def multiply_step(s):
-            r, g = divmod(s, PASSES)
+        def transpose_round(r):
+            codes = quantised_pool.tile([P, PASSES * P], U32, align_bytes=64)
+            scales = quantised_pool.tile([P, PASSES * P], U8, align_bytes=64)
+            quantised[r] = (codes, scales)
+            for c in range(STEPS):
+                transpose_step(r, c)
+                if c >= 1:
+                    quantise_step(r, c - 1)
+                elif r >= 1:
+                    quantise_step(r - 1, STEPS - 1)
+            if r + G_BUFS < ROUNDS:
+                g_words[r + G_BUFS] = load_round(r + G_BUFS)
+
+        def multiply_round(r):
             codes, scales = quantised[r]
-            if g == 0:
-                acc_of[r] = [sums.tile([P, D], F32, name="acc%d" % j) for j in range(ROW_TILES)]
-            acc = acc_of[r]
-            h_cols = slice(g * D, (g + 1) * D)
-            for j in range(ROW_TILES):
+            acc = sums.tile([P, D], F32)
+            for g in range(PASSES):
+                cols = slice(g * P, (g + 1) * P)
                 nc.tensor.matmul_mx(
-                    out=acc[j][:],
-                    lhsT=codes[:, operand_cols(g, j)].bitcast(FP8X4),
-                    lhsT_scale=scales[:, operand_cols(g, j)],
-                    rhs=h_codes[:, h_cols].bitcast(FP8X4),
-                    rhs_scale=h_scales[:, h_cols],
+                    out=acc[:],
+                    lhsT=codes[:, cols].bitcast(FP8X4),
+                    lhsT_scale=scales[:, cols],
+                    rhs=h_codes[:, cols].bitcast(FP8X4),
+                    rhs_scale=h_scales[:, cols],
                     start=(g == 0),
                     stop=(g == PASSES - 1),
                 )
-            if g == PASSES - 1:
-                z = z_pool.tile([P, ROW_TILES, D], F32)
-                nc.vector.tensor_copy(out=z[:, 0, :], in_=acc[0][:])
-                nc.scalar.copy(out=z[:, 1, :], in_=acc[1][:])
-                rows = slice(r * ROUND_ROWS, (r + 1) * ROUND_ROWS)
-                nc.sync.dma_start(
-                    out=out[rows, :].rearrange("(p j) d -> p j d", j=ROW_TILES), in_=z[:]
-                )
+            z = z_pool.tile([P, D], F32)
+            copy_out(r % 2 == 1, z[:], acc[:])
+            nc.sync.dma_start(out=out[r * P : (r + 1) * P, :], in_=z[:])
 
-        for run in range(RUNS + 1):
-            if run < RUNS:
-                for s in range(run * RUN_STEPS, (run + 1) * RUN_STEPS):
-                    transpose_step(s)
-                    if s >= 1:
-                        quantise_step(s - 1)
-            else:
-                quantise_step(STEPS - 1)
-            if run >= 1:
-                for s in range((run - 1) * RUN_STEPS, run * RUN_STEPS):
-                    multiply_step(s)
+        for r in range(ROUNDS):
+            transpose_round(r)
+            if r >= 1:
+                multiply_round(r - 1)
+        quantise_step(ROUNDS - 1, STEPS - 1)
+        multiply_round(ROUNDS - 1)

from contextlib import ExitStack

import concourse.mybir as mybir
from concourse.masks import make_identity

BF16 = mybir.dt.bfloat16
F32 = mybir.dt.float32
U32 = mybir.dt.uint32
U8 = mybir.dt.uint8
FP8X4 = mybir.dt.float8_e4m3fn_x4

P = 128
PACK = 4
K_PASS = P * PACK
N_E, N_F, D = 3072, 2048, 128
E_PASSES = N_E // K_PASS
F_PASSES = N_F // K_PASS
PASSES = E_PASSES + F_PASSES
WORDS_PASS = K_PASS // 2
ROUNDS = N_F // P

STEP_PASSES = 2
STEPS = PASSES // STEP_PASSES
STEP_COLS = STEP_PASSES * K_PASS
STEP_WORDS = STEP_COLS // PACK

X_AHEAD = 2
G_BUFS = 14
WORK_BANKS = 6

FLOPS = 2 * N_F * (N_E + N_F) * D + 2 * (N_E + N_F) * D * D


def tile_two_d_cxn_cmps_pb_kernel(tc, xe, xf, Ge2f, Gf2f, We2f, Wf2f, out):
    nc = tc.nc
    with ExitStack() as stack:
        keep = stack.enter_context(tc.tile_pool(name="keep", bufs=1))
        g_pool = stack.enter_context(tc.tile_pool(name="g", bufs=G_BUFS))
        grouped_pool = stack.enter_context(tc.tile_pool(name="grouped", bufs=6))
        quantised_pool = stack.enter_context(tc.tile_pool(name="quantised", bufs=4))
        z_pool = stack.enter_context(tc.tile_pool(name="z", bufs=ROUNDS))
        work = stack.enter_context(tc.psum_pool(name="work", bufs=WORK_BANKS))
        sums = stack.enter_context(tc.psum_pool(name="sums", bufs=2))
        stack.enter_context(tc.manual_schedule())

        we_sb = keep.tile([P, D], BF16)
        nc.sync.dma_start(out=we_sb[:], in_=We2f)
        wf_sb = keep.tile([P, D], BF16)
        nc.sync.dma_start(out=wf_sb[:], in_=Wf2f)
        x_sb = keep.tile([P, PASSES * PACK, D], BF16)
        x_pairs = x_sb[:].rearrange("p (a e) d -> p a e d", e=2)
        for x_dram, first_pass, passes in ((xe, 0, E_PASSES), (xf, E_PASSES, F_PASSES)):
            pairs_dram = x_dram.rearrange("(a p e) d -> p a e d", p=P, e=2)
            for g in range(0, passes, STEP_PASSES):
                nc.sync.dma_start(
                    out=x_pairs[:, 2 * (first_pass + g) : 2 * (first_pass + g + STEP_PASSES)],
                    in_=pairs_dram[:, 2 * g : 2 * (g + STEP_PASSES)],
                )

        def load_round(r):
            rows = slice(r * P, (r + 1) * P)
            ge = g_pool.tile([P, N_E], BF16)
            nc.sync.dma_start(out=ge[:], in_=Ge2f[rows, :])
            gf = g_pool.tile([P, N_F], BF16)
            nc.sync.dma_start(out=gf[:], in_=Gf2f[rows, :])
            return ge[:].bitcast(F32), gf[:].bitcast(F32)

        g_words = {}
        for r in range(G_BUFS):
            g_words[r] = load_round(r)

        ident_bf16 = keep.tile([P, P], BF16)
        make_identity(nc, ident_bf16[:])
        ident_f32 = keep.tile([P, P], F32)
        make_identity(nc, ident_f32[:])

        xT_sb = keep.tile([P, PASSES, PACK, P], BF16)
        h_grouped = keep.tile([P, PASSES, D, PACK], BF16, align_bytes=64)
        h_codes = keep.tile([P, PASSES * D], U32, align_bytes=64)
        h_scales = keep.tile([P, PASSES * D], U8, align_bytes=64)

        def copy_out(on_scalar, dst, src):
            if on_scalar:
                nc.scalar.copy(out=dst, in_=src)
            else:
                nc.vector.tensor_copy(out=dst, in_=src)

        def transpose_x(g):
            xT_bank = work.tile([P, PACK, P], BF16, tag="bank")
            for t in range(PACK):
                nc.tensor.transpose(xT_bank[:, t, :], x_sb[:, PACK * g + t, :], ident_bf16[:])
            copy_out(g % 2 == 0, xT_sb[:, g], xT_bank[:])

        def multiply_x(g):
            w_sb = we_sb if g < E_PASSES else wf_sb
            h_bank = work.tile([P, PACK, D], F32, tag="bank")
            for t in range(PACK):
                nc.tensor.matmul(
                    h_bank[:, t, :], lhsT=xT_sb[:, g, t, :], rhs=w_sb[:], start=True, stop=True
                )
            copy_out(g % 2 == 1, h_grouped[:, g], h_bank[:].rearrange("p t d -> p d t"))

        def quantise_h(c):
            cols = slice(c * STEP_WORDS, (c + 1) * STEP_WORDS)
            nc.vector.quantize_mx(
                out=h_codes[:, cols].bitcast(FP8X4),
                scales=h_scales[:, cols],
                in_=h_grouped[:, c * STEP_PASSES : (c + 1) * STEP_PASSES].rearrange(
                    "p g d t -> p (g d t)"
                ),
            )

        for g in range(X_AHEAD):
            transpose_x(g)
        for g in range(PASSES):
            if g + X_AHEAD < PASSES:
                transpose_x(g + X_AHEAD)
            multiply_x(g)
            if g % STEP_PASSES == STEP_PASSES - 1 and g // STEP_PASSES >= 1:
                quantise_h(g // STEP_PASSES - 1)
        quantise_h(STEPS - 1)

        quantised = {}
        grouped_of = {}

        def transpose_step(r, c):
            ge_words, gf_words = g_words[r]
            bank = work.tile([P, STEP_PASSES, 2, P], F32, tag="bank")
            for i in range(STEP_PASSES):
                g = c * STEP_PASSES + i
                words, g_local = (ge_words, g) if g < E_PASSES else (gf_words, g - E_PASSES)
                for u in range(2):
                    first = g_local * WORDS_PASS + u * P
                    nc.tensor.transpose(bank[:, i, u, :], words[:, first : first + P], ident_f32[:])
            grouped = grouped_pool.tile([P, STEP_COLS], BF16, align_bytes=64)
            grouped_of[(r, c)] = grouped
            dst = grouped[:].bitcast(F32).rearrange("p (i r u) -> p i r u", i=STEP_PASSES, u=2)
            copy_out(c != 0, dst, bank[:].rearrange("p i u r -> p i r u"))

        def quantise_step(r, c):
            codes, scales = quantised[r]
            cols = slice(c * STEP_WORDS, (c + 1) * STEP_WORDS)
            nc.vector.quantize_mx(
                out=codes[:, cols].bitcast(FP8X4), scales=scales[:, cols], in_=grouped_of[(r, c)][:]
            )

        def transpose_round(r):
            codes = quantised_pool.tile([P, PASSES * P], U32, align_bytes=64)
            scales = quantised_pool.tile([P, PASSES * P], U8, align_bytes=64)
            quantised[r] = (codes, scales)
            for c in range(STEPS):
                transpose_step(r, c)
                if c >= 1:
                    quantise_step(r, c - 1)
                elif r >= 1:
                    quantise_step(r - 1, STEPS - 1)
            if r + G_BUFS < ROUNDS:
                g_words[r + G_BUFS] = load_round(r + G_BUFS)

        def multiply_round(r):
            codes, scales = quantised[r]
            acc = sums.tile([P, D], F32)
            for g in range(PASSES):
                cols = slice(g * P, (g + 1) * P)
                nc.tensor.matmul_mx(
                    out=acc[:],
                    lhsT=codes[:, cols].bitcast(FP8X4),
                    lhsT_scale=scales[:, cols],
                    rhs=h_codes[:, cols].bitcast(FP8X4),
                    rhs_scale=h_scales[:, cols],
                    start=(g == 0),
                    stop=(g == PASSES - 1),
                )
            z = z_pool.tile([P, D], F32)
            copy_out(r % 2 == 1, z[:], acc[:])
            nc.sync.dma_start(out=out[r * P : (r + 1) * P, :], in_=z[:])

        for r in range(ROUNDS):
            transpose_round(r)
            if r >= 1:
                multiply_round(r - 1)
        quantise_step(ROUNDS - 1, STEPS - 1)
        multiply_round(ROUNDS - 1)
